import numpy as np
import ml_dtypes


def mxq(x, axis, fmt="e4m3"):
    dtype, down = {"e4m3": (ml_dtypes.float8_e4m3fn, 7), "e5m2": (ml_dtypes.float8_e5m2, 14)}[fmt]
    v = np.moveaxis(np.asarray(x, np.float32).astype(ml_dtypes.bfloat16).astype(np.float64), axis, -1)
    blocks = v.reshape(v.shape[:-1] + (-1, 32))
    amax = np.abs(blocks).max(-1, keepdims=True)
    byte = np.maximum(np.where(amax > 0, np.frexp(amax)[1] - 1 + 127, 0) - down, 1)
    scale = np.exp2(byte - 127.0)
    codes = (blocks / scale).astype(np.float32).astype(dtype).astype(np.float64)
    return np.moveaxis((codes * scale).reshape(v.shape), -1, axis)


WIDE = False


def mx_kscale(k):
    if not WIDE:
        return np.ones(k)
    levels = np.array([20, -20, 10, -10, 0])
    a = np.random.permutation(np.resize(levels, k // 512 * 4)).reshape(k // 512, 4)
    idx = np.arange(k)
    return np.exp2(a[idx // 512, idx % 128 // 32])


BF16 = ml_dtypes.bfloat16


def bf(x):
    return np.asarray(x, np.float32).astype(BF16)


def f64(x):
    return np.asarray(x).astype(np.float64)


B, IN, OUT, R, Q, ORD = 512, 1024, 1024, 8, 16384, 3
K = R ** ORD


def setup_inputs():
    s = mx_kscale(Q)[:, None]
    z = np.random.standard_normal((ORD, R, B))
    g2 = np.random.standard_normal((Q, K)) / np.sqrt(K) / s
    g = np.random.standard_normal((Q, B)) * np.exp2(np.random.randint(-12, 1, (1, B))) * s
    return {"z": bf(z), "G2": bf(g2), "grad_out": bf(g)}


def reference(z, G2, grad_out):
    Z = f64(z)
    dk = mxq(f64(G2), 0, "e4m3").T @ mxq(f64(grad_out), 0, "e5m2")
    D = dk.reshape((R, R, R, B))
    t = (D * Z[2][:, None, None, :]).sum(axis=0)
    d0 = (t * Z[1][:, None, :]).sum(axis=0)
    d1 = (t * Z[0][None, :, :]).sum(axis=1)
    u = (D * Z[0][None, None, :, :]).sum(axis=2)
    d2 = (u * Z[1][None, :, :]).sum(axis=1)
    return np.stack([d0, d1, d2], axis=0)

@@ -1,0 +1,170 @@
+from contextlib import ExitStack
+
+import concourse.mybir as mybir
+from concourse.masks import make_identity
+
+BF16 = mybir.dt.bfloat16
+F32 = mybir.dt.float32
+U32 = mybir.dt.uint32
+U8 = mybir.dt.uint8
+E4M3X4 = mybir.dt.float8_e4m3fn_x4
+E5M2X4 = mybir.dt.float8_e5m2_x4
+MULT = mybir.AluOpType.mult
+ADD = mybir.AluOpType.add
+X = mybir.AxisListType.X
+
+P = 128
+PACK = 4
+K_PASS = P * PACK
+Q = 16384
+PASSES = Q // K_PASS
+R = 8
+ORD = 3
+KRON = R**ORD
+B = 512
+N_TILES = B // P
+RUN = 4
+
+FLOPS = 2 * Q * KRON * B
+
+
+def regroup(copy, raw, grouped):
+    copy(
+        out=grouped[:].rearrange("p (g i) t -> p g t i", i=RUN),
+        in_=raw[:].rearrange("p t (g i) -> p g t i", i=RUN),
+    )
+
+
+def tile_fast_tucker_taylor_pa_k_kernel(tc, z, G2, grad_out, out):
+    nc = tc.nc
+    with ExitStack() as ctx:
+        const = ctx.enter_context(tc.tile_pool(name="const", bufs=1))
+        raw_pool = ctx.enter_context(tc.tile_pool(name="raw", bufs=8))
+        grouped_pool = ctx.enter_context(tc.tile_pool(name="grouped", bufs=3))
+        mx_pool = ctx.enter_context(tc.tile_pool(name="mx", bufs=3))
+        tail = ctx.enter_context(tc.tile_pool(name="tail", bufs=1))
+        psum = ctx.enter_context(tc.psum_pool(name="psum", bufs=1))
+
+        ident_bf = const.tile([P, P], BF16)
+        make_identity(nc, ident_bf[:])
+        ident_f32 = const.tile([P, P], F32)
+        make_identity(nc, ident_f32[:])
+        z_rows = const.tile([P, B], BF16)
+        nc.vector.memset(z_rows[:], 0.0)
+        nc.scalar.dma_start(out=z_rows[0 : ORD * R, :], in_=z.rearrange("o r n -> (o r) n"))
+        zT_ps = psum.tile([P, N_TILES, P], BF16)
+        for j in range(N_TILES):
+            nc.tensor.transpose(zT_ps[:, j, :], z_rows[:, j * P : (j + 1) * P], ident_bf[:])
+        zT = const.tile([P, N_TILES, ORD * R], F32)
+        nc.vector.tensor_copy(out=zT[:], in_=zT_ps[:, :, 0 : ORD * R])
+        z0 = zT[:, :, 0:R]
+        z1 = zT[:, :, R : 2 * R]
+        z2 = zT[:, :, 2 * R : 3 * R]
+
+        res = tail.tile([P, P], F32)
+        nc.vector.memset(res[:], 0.0)
+
+        acc = [psum.tile([P, KRON], F32, name="acc%d" % j) for j in range(N_TILES)]
+
+        def load_and_regroup(c):
+            rows = slice(c * K_PASS, (c + 1) * K_PASS)
+            g_raw = raw_pool.tile([P, PACK, B], BF16)
+            nc.sync.dma_start(out=g_raw[:], in_=grad_out[rows, :].rearrange("(p t) w -> p t w", t=PACK))
+            w_raw = raw_pool.tile([P, PACK, KRON], BF16)
+            nc.sync.dma_start(out=w_raw[:], in_=G2[rows, :].rearrange("(p t) w -> p t w", t=PACK))
+            g_grouped = grouped_pool.tile([P, B, PACK], BF16, align_bytes=64)
+            regroup(nc.scalar.copy, g_raw, g_grouped)
+            w_grouped = grouped_pool.tile([P, KRON, PACK], BF16, align_bytes=64)
+            regroup(nc.vector.tensor_copy, w_raw, w_grouped)
+            return g_grouped, w_grouped
+
+        def quantise_and_multiply(c, g_grouped, w_grouped):
+            g_codes = mx_pool.tile([P, B], U32, align_bytes=64)
+            g_scales = mx_pool.tile([P, B], U8, align_bytes=64)
+            nc.vector.quantize_mx(
+                out=g_codes[:].bitcast(E5M2X4),
+                scales=g_scales[:],
+                in_=g_grouped[:].rearrange("p w t -> p (w t)"),
+            )
+            w_codes = mx_pool.tile([P, KRON], U32, align_bytes=64)
+            w_scales = mx_pool.tile([P, KRON], U8, align_bytes=64)
+            nc.vector.quantize_mx(
+                out=w_codes[:].bitcast(E4M3X4),
+                scales=w_scales[:],
+                in_=w_grouped[:].rearrange("p w t -> p (w t)"),
+            )
+            for j in range(N_TILES):
+                n_cols = slice(j * P, (j + 1) * P)
+                nc.tensor.matmul_mx(
+                    out=acc[j][:],
+                    lhsT=g_codes[:, n_cols].bitcast(E5M2X4),
+                    lhsT_scale=g_scales[:, n_cols],
+                    rhs=w_codes[:].bitcast(E4M3X4),
+                    rhs_scale=w_scales[:],
+                    start=(c == 0),
+                    stop=(c == PASSES - 1),
+                )
+
+        grouped = load_and_regroup(0)
+        for c in range(1, PASSES):
+            grouped_next = load_and_regroup(c)
+            quantise_and_multiply(c - 1, grouped[0], grouped[1])
+            grouped = grouped_next
+        quantise_and_multiply(PASSES - 1, grouped[0], grouped[1])
+
+        prod_a = tail.tile([P, N_TILES, R * R, R], F32)
+        prod_c = tail.tile([P, N_TILES, R * R, R], F32)
+        for j in range(N_TILES):
+            nc.vector.tensor_tensor(
+                out=prod_a[:, j],
+                in0=acc[j][:].rearrange("p (f a) -> p f a", a=R),
+                in1=z0[:, j].unsqueeze(1).to_broadcast([P, R * R, R]),
+                op=MULT,
+            )
+        for j in range(N_TILES):
+            nc.vector.tensor_tensor(
+                out=prod_c[:, j],
+                in0=acc[j][:].rearrange("p (c f) -> p f c", c=R),
+                in1=z2[:, j].unsqueeze(1).to_broadcast([P, R * R, R]),
+                op=MULT,
+            )
+        u = tail.tile([P, N_TILES, R, R], F32)
+        nc.vector.tensor_reduce(
+            out=u[:].rearrange("p j c b -> p (j c b)"),
+            in_=prod_a[:].rearrange("p j f a -> p (j f) a"),
+            axis=X,
+            op=ADD,
+        )
+        t = tail.tile([P, N_TILES, R, R], F32)
+        nc.vector.tensor_reduce(
+            out=t[:].rearrange("p j b a -> p (j b a)"),
+            in_=prod_c[:].rearrange("p j f c -> p (j f) c"),
+            axis=X,
+            op=ADD,
+        )
+
+        shape = [P, N_TILES, R, R]
+        pair2 = tail.tile(shape, F32)
+        nc.vector.tensor_tensor(out=pair2[:], in0=u[:], in1=z1.unsqueeze(2).to_broadcast(shape), op=MULT)
+        pair1 = tail.tile(shape, F32)
+        nc.vector.tensor_tensor(out=pair1[:], in0=t[:], in1=z0.unsqueeze(2).to_broadcast(shape), op=MULT)
+        pair0 = tail.tile(shape, F32)
+        nc.vector.tensor_tensor(
+            out=pair0[:],
+            in0=t[:].rearrange("p j b a -> p j a b"),
+            in1=z1.unsqueeze(2).to_broadcast(shape),
+            op=MULT,
+        )
+        res_ojr = res[:, 0 : ORD * R * N_TILES].rearrange("p (o r j) -> p o j r", o=ORD, j=N_TILES)
+        nc.vector.tensor_reduce(out=res_ojr[:, 2], in_=pair2[:], axis=X, op=ADD)
+        nc.vector.tensor_reduce(out=res_ojr[:, 1], in_=pair1[:], axis=X, op=ADD)
+        nc.vector.tensor_reduce(out=res_ojr[:, 0], in_=pair0[:], axis=X, op=ADD)
+
+        resT_ps = psum.tile([P, P], F32)
+        nc.tensor.transpose(resT_ps[:], res[:], ident_f32[:])
+        resT = tail.tile([P, P], F32)
+        nc.vector.tensor_copy(out=resT[:], in_=resT_ps[:])
+        nc.sync.dma_start(
+            out=out.rearrange("o r (j n) -> (o r j) n", j=N_TILES),
+            in_=resT[0 : ORD * R * N_TILES, :],
+        )

@@ -12,6 +12,7 @@ E5M2X4 = mybir.dt.float8_e5m2_x4
 MULT = mybir.AluOpType.mult
 ADD = mybir.AluOpType.add
 X = mybir.AxisListType.X
+COPY = mybir.ActivationFunctionType.Copy
 
 P = 128
 PACK = 4
@@ -66,19 +67,18 @@ def tile_fast_tucker_taylor_pa_k_kernel(tc, z, G2, grad_out, out):
 
         acc = [psum.tile([P, KRON], F32, name="acc%d" % j) for j in range(N_TILES)]
 
-        def load_and_regroup(c):
+        for c in range(PASSES):
             rows = slice(c * K_PASS, (c + 1) * K_PASS)
             g_raw = raw_pool.tile([P, PACK, B], BF16)
             nc.sync.dma_start(out=g_raw[:], in_=grad_out[rows, :].rearrange("(p t) w -> p t w", t=PACK))
             w_raw = raw_pool.tile([P, PACK, KRON], BF16)
             nc.sync.dma_start(out=w_raw[:], in_=G2[rows, :].rearrange("(p t) w -> p t w", t=PACK))
+
             g_grouped = grouped_pool.tile([P, B, PACK], BF16, align_bytes=64)
             regroup(nc.scalar.copy, g_raw, g_grouped)
             w_grouped = grouped_pool.tile([P, KRON, PACK], BF16, align_bytes=64)
             regroup(nc.vector.tensor_copy, w_raw, w_grouped)
-            return g_grouped, w_grouped
 
-        def quantise_and_multiply(c, g_grouped, w_grouped):
             g_codes = mx_pool.tile([P, B], U32, align_bytes=64)
             g_scales = mx_pool.tile([P, B], U8, align_bytes=64)
             nc.vector.quantize_mx(
@@ -105,29 +105,32 @@ def tile_fast_tucker_taylor_pa_k_kernel(tc, z, G2, grad_out, out):
                     stop=(c == PASSES - 1),
                 )
 
-        grouped = load_and_regroup(0)
-        for c in range(1, PASSES):
-            grouped_next = load_and_regroup(c)
-            quantise_and_multiply(c - 1, grouped[0], grouped[1])
-            grouped = grouped_next
-        quantise_and_multiply(PASSES - 1, grouped[0], grouped[1])
-
         prod_a = tail.tile([P, N_TILES, R * R, R], F32)
-        prod_c = tail.tile([P, N_TILES, R * R, R], F32)
-        for j in range(N_TILES):
+        scaled = tail.tile([P, N_TILES, R, R * R], F32)
+        t_ps = psum.tile([P, N_TILES, R, R], F32)
+        for i in range(N_TILES):
+            j = (i + 1) % N_TILES
             nc.vector.tensor_tensor(
                 out=prod_a[:, j],
                 in0=acc[j][:].rearrange("p (f a) -> p f a", a=R),
                 in1=z0[:, j].unsqueeze(1).to_broadcast([P, R * R, R]),
                 op=MULT,
             )
-        for j in range(N_TILES):
-            nc.vector.tensor_tensor(
-                out=prod_c[:, j],
-                in0=acc[j][:].rearrange("p (c f) -> p f c", c=R),
-                in1=z2[:, j].unsqueeze(1).to_broadcast([P, R * R, R]),
-                op=MULT,
-            )
+            j = i
+            for c in range(R):
+                nc.scalar.activation(
+                    out=scaled[:, j, c],
+                    in_=acc[j][:, c * R * R : (c + 1) * R * R],
+                    func=COPY,
+                    scale=z2[:, j, c : c + 1],
+                )
+                nc.tensor.matmul(
+                    out=t_ps[:, j].rearrange("p b a -> p (b a)"),
+                    lhsT=ident_f32[:],
+                    rhs=scaled[:, j, c],
+                    start=(c == 0),
+                    stop=(c == R - 1),
+                )
         u = tail.tile([P, N_TILES, R, R], F32)
         nc.vector.tensor_reduce(
             out=u[:].rearrange("p j c b -> p (j c b)"),
@@ -135,30 +138,33 @@ def tile_fast_tucker_taylor_pa_k_kernel(tc, z, G2, grad_out, out):
             axis=X,
             op=ADD,
         )
-        t = tail.tile([P, N_TILES, R, R], F32)
-        nc.vector.tensor_reduce(
-            out=t[:].rearrange("p j b a -> p (j b a)"),
-            in_=prod_c[:].rearrange("p j f c -> p (j f) c"),
-            axis=X,
-            op=ADD,
-        )
 
+        pairs = tail.tile([P, ORD, R, N_TILES, R], F32)
         shape = [P, N_TILES, R, R]
-        pair2 = tail.tile(shape, F32)
-        nc.vector.tensor_tensor(out=pair2[:], in0=u[:], in1=z1.unsqueeze(2).to_broadcast(shape), op=MULT)
-        pair1 = tail.tile(shape, F32)
-        nc.vector.tensor_tensor(out=pair1[:], in0=t[:], in1=z0.unsqueeze(2).to_broadcast(shape), op=MULT)
-        pair0 = tail.tile(shape, F32)
         nc.vector.tensor_tensor(
-            out=pair0[:],
-            in0=t[:].rearrange("p j b a -> p j a b"),
+            out=pairs[:, 2].rearrange("p c j b -> p j c b"),
+            in0=u[:],
             in1=z1.unsqueeze(2).to_broadcast(shape),
             op=MULT,
         )
-        res_ojr = res[:, 0 : ORD * R * N_TILES].rearrange("p (o r j) -> p o j r", o=ORD, j=N_TILES)
-        nc.vector.tensor_reduce(out=res_ojr[:, 2], in_=pair2[:], axis=X, op=ADD)
-        nc.vector.tensor_reduce(out=res_ojr[:, 1], in_=pair1[:], axis=X, op=ADD)
-        nc.vector.tensor_reduce(out=res_ojr[:, 0], in_=pair0[:], axis=X, op=ADD)
+        nc.vector.tensor_tensor(
+            out=pairs[:, 1].rearrange("p b j c -> p j b c"),
+            in0=u[:].rearrange("p j c b -> p j b c"),
+            in1=z2.unsqueeze(2).to_broadcast(shape),
+            op=MULT,
+        )
+        nc.vector.tensor_tensor(
+            out=pairs[:, 0].rearrange("p a j b -> p j a b"),
+            in0=t_ps[:].rearrange("p j b a -> p j a b"),
+            in1=z1.unsqueeze(2).to_broadcast(shape),
+            op=MULT,
+        )
+        nc.vector.tensor_reduce(
+            out=res[:, 0 : ORD * R * N_TILES],
+            in_=pairs[:].rearrange("p o r j y -> p (o r j) y"),
+            axis=X,
+            op=ADD,
+        )
 
         resT_ps = psum.tile([P, P], F32)
         nc.tensor.transpose(resT_ps[:], res[:], ident_f32[:])

@@ -39,10 +39,11 @@ def regroup(copy, raw, grouped):
 def tile_fast_tucker_taylor_pa_k_kernel(tc, z, G2, grad_out, out):
     nc = tc.nc
     with ExitStack() as ctx:
+        ctx.enter_context(tc.manual_schedule())
         const = ctx.enter_context(tc.tile_pool(name="const", bufs=1))
         raw_pool = ctx.enter_context(tc.tile_pool(name="raw", bufs=8))
-        grouped_pool = ctx.enter_context(tc.tile_pool(name="grouped", bufs=3))
-        mx_pool = ctx.enter_context(tc.tile_pool(name="mx", bufs=3))
+        grouped_pool = ctx.enter_context(tc.tile_pool(name="grouped", bufs=5))
+        mx_pool = ctx.enter_context(tc.tile_pool(name="mx", bufs=5))
         tail = ctx.enter_context(tc.tile_pool(name="tail", bufs=1))
         psum = ctx.enter_context(tc.psum_pool(name="psum", bufs=1))
 
@@ -56,11 +57,6 @@ def tile_fast_tucker_taylor_pa_k_kernel(tc, z, G2, grad_out, out):
         zT_ps = psum.tile([P, N_TILES, P], BF16)
         for j in range(N_TILES):
             nc.tensor.transpose(zT_ps[:, j, :], z_rows[:, j * P : (j + 1) * P], ident_bf[:])
-        zT = const.tile([P, N_TILES, ORD * R], F32)
-        nc.vector.tensor_copy(out=zT[:], in_=zT_ps[:, :, 0 : ORD * R])
-        z0 = zT[:, :, 0:R]
-        z1 = zT[:, :, R : 2 * R]
-        z2 = zT[:, :, 2 * R : 3 * R]
 
         res = tail.tile([P, P], F32)
         nc.vector.memset(res[:], 0.0)
@@ -105,9 +101,14 @@ def tile_fast_tucker_taylor_pa_k_kernel(tc, z, G2, grad_out, out):
                     stop=(c == PASSES - 1),
                 )
 
+        zT = const.tile([P, N_TILES, ORD * R], F32)
+        nc.scalar.copy(out=zT[:], in_=zT_ps[:, :, 0 : ORD * R])
+        z0 = zT[:, :, 0:R]
+        z1 = zT[:, :, R : 2 * R]
+        z2 = zT[:, :, 2 * R : 3 * R]
+
         prod_a = tail.tile([P, N_TILES, R * R, R], F32)
         scaled = tail.tile([P, N_TILES, R, R * R], F32)
-        t_ps = psum.tile([P, N_TILES, R, R], F32)
         for i in range(N_TILES):
             j = (i + 1) % N_TILES
             nc.vector.tensor_tensor(
@@ -124,13 +125,6 @@ def tile_fast_tucker_taylor_pa_k_kernel(tc, z, G2, grad_out, out):
                     func=COPY,
                     scale=z2[:, j, c : c + 1],
                 )
-                nc.tensor.matmul(
-                    out=t_ps[:, j].rearrange("p b a -> p (b a)"),
-                    lhsT=ident_f32[:],
-                    rhs=scaled[:, j, c],
-                    start=(c == 0),
-                    stop=(c == R - 1),
-                )
         u = tail.tile([P, N_TILES, R, R], F32)
         nc.vector.tensor_reduce(
             out=u[:].rearrange("p j c b -> p (j c b)"),
@@ -138,6 +132,16 @@ def tile_fast_tucker_taylor_pa_k_kernel(tc, z, G2, grad_out, out):
             axis=X,
             op=ADD,
         )
+        pieces = R
+        while pieces > 1:
+            pieces = pieces // 2
+            nc.vector.tensor_tensor(
+                out=scaled[:, :, 0:pieces],
+                in0=scaled[:, :, 0:pieces],
+                in1=scaled[:, :, pieces : 2 * pieces],
+                op=ADD,
+            )
+        t = scaled[:, :, 0].rearrange("p j (b a) -> p j b a", a=R)
 
         pairs = tail.tile([P, ORD, R, N_TILES, R], F32)
         shape = [P, N_TILES, R, R]
@@ -155,7 +159,7 @@ def tile_fast_tucker_taylor_pa_k_kernel(tc, z, G2, grad_out, out):
         )
         nc.vector.tensor_tensor(
             out=pairs[:, 0].rearrange("p a j b -> p j a b"),
-            in0=t_ps[:].rearrange("p j b a -> p j a b"),
+            in0=t.rearrange("p j b a -> p j a b"),
             in1=z1.unsqueeze(2).to_broadcast(shape),
             op=MULT,
         )

@@ -24,6 +24,9 @@ ORD = 3
 KRON = R**ORD
 B = 512
 N_TILES = B // P
+G_PE = 112
+W_PE = 80
+G_SBUF = B - G_PE
 RUN = 4
 
 FLOPS = 2 * Q * KRON * B
@@ -31,9 +34,20 @@ FLOPS = 2 * Q * KRON * B
 
 def regroup(copy, raw, grouped):
     copy(
-        out=grouped[:].rearrange("p (g i) t -> p g t i", i=RUN),
-        in_=raw[:].rearrange("p t (g i) -> p g t i", i=RUN),
+        out=grouped.rearrange("p (g i) t -> p g t i", i=RUN),
+        in_=raw.rearrange("p t (g i) -> p g t i", i=RUN),
     )
+
+
+def regroup_on_tensor(nc, ident, raw, grouped):
+    for t in range(0, PACK, 2):
+        nc.tensor.matmul(
+            out=grouped[:, :, t : t + 2],
+            lhsT=ident,
+            rhs=raw[:, t : t + 2, :].rearrange("p t w -> p w t"),
+            start=True,
+            stop=True,
+        )
 
 
 def tile_fast_tucker_taylor_pa_k_kernel(tc, z, G2, grad_out, out):
@@ -46,6 +60,7 @@ def tile_fast_tucker_taylor_pa_k_kernel(tc, z, G2, grad_out, out):
         mx_pool = ctx.enter_context(tc.tile_pool(name="mx", bufs=5))
         tail = ctx.enter_context(tc.tile_pool(name="tail", bufs=1))
         psum = ctx.enter_context(tc.psum_pool(name="psum", bufs=1))
+        move_psum = ctx.enter_context(tc.psum_pool(name="move_psum", bufs=2))
 
         ident_bf = const.tile([P, P], BF16)
         make_identity(nc, ident_bf[:])
@@ -63,32 +78,7 @@ def tile_fast_tucker_taylor_pa_k_kernel(tc, z, G2, grad_out, out):
 
         acc = [psum.tile([P, KRON], F32, name="acc%d" % j) for j in range(N_TILES)]
 
-        for c in range(PASSES):
-            rows = slice(c * K_PASS, (c + 1) * K_PASS)
-            g_raw = raw_pool.tile([P, PACK, B], BF16)
-            nc.sync.dma_start(out=g_raw[:], in_=grad_out[rows, :].rearrange("(p t) w -> p t w", t=PACK))
-            w_raw = raw_pool.tile([P, PACK, KRON], BF16)
-            nc.sync.dma_start(out=w_raw[:], in_=G2[rows, :].rearrange("(p t) w -> p t w", t=PACK))
-
-            g_grouped = grouped_pool.tile([P, B, PACK], BF16, align_bytes=64)
-            regroup(nc.scalar.copy, g_raw, g_grouped)
-            w_grouped = grouped_pool.tile([P, KRON, PACK], BF16, align_bytes=64)
-            regroup(nc.vector.tensor_copy, w_raw, w_grouped)
-
-            g_codes = mx_pool.tile([P, B], U32, align_bytes=64)
-            g_scales = mx_pool.tile([P, B], U8, align_bytes=64)
-            nc.vector.quantize_mx(
-                out=g_codes[:].bitcast(E5M2X4),
-                scales=g_scales[:],
-                in_=g_grouped[:].rearrange("p w t -> p (w t)"),
-            )
-            w_codes = mx_pool.tile([P, KRON], U32, align_bytes=64)
-            w_scales = mx_pool.tile([P, KRON], U8, align_bytes=64)
-            nc.vector.quantize_mx(
-                out=w_codes[:].bitcast(E4M3X4),
-                scales=w_scales[:],
-                in_=w_grouped[:].rearrange("p w t -> p (w t)"),
-            )
+        def multiply(c, g_codes, g_scales, w_codes, w_scales):
             for j in range(N_TILES):
                 n_cols = slice(j * P, (j + 1) * P)
                 nc.tensor.matmul_mx(
@@ -100,6 +90,42 @@ def tile_fast_tucker_taylor_pa_k_kernel(tc, z, G2, grad_out, out):
                     start=(c == 0),
                     stop=(c == PASSES - 1),
                 )
+
+        operands = None
+        for c in range(PASSES):
+            rows = slice(c * K_PASS, (c + 1) * K_PASS)
+            g_raw = raw_pool.tile([P, PACK, B], BF16)
+            nc.sync.dma_start(out=g_raw[:], in_=grad_out[rows, :].rearrange("(p t) w -> p t w", t=PACK))
+            w_raw = raw_pool.tile([P, PACK, KRON], BF16)
+            nc.sync.dma_start(out=w_raw[:], in_=G2[rows, :].rearrange("(p t) w -> p t w", t=PACK))
+
+            grouped = grouped_pool.tile([P, B + KRON, PACK], BF16, align_bytes=64)
+            moved = move_psum.tile([P, G_PE + W_PE, PACK], BF16)
+            regroup_on_tensor(nc, ident_bf[:], g_raw[:, :, G_SBUF:B], moved[:, 0:G_PE])
+            regroup_on_tensor(nc, ident_bf[:], w_raw[:, :, 0:W_PE], moved[:, G_PE : G_PE + W_PE])
+            if c > 0:
+                multiply(c - 1, *operands)
+
+            regroup(nc.scalar.copy, g_raw[:, :, 0:G_SBUF], grouped[:, 0:G_SBUF])
+            nc.scalar.copy(out=grouped[:, G_SBUF : B + W_PE], in_=moved[:])
+            regroup(nc.vector.tensor_copy, w_raw[:, :, W_PE:KRON], grouped[:, B + W_PE : B + KRON])
+
+            g_codes = mx_pool.tile([P, B], U32, align_bytes=64)
+            g_scales = mx_pool.tile([P, B], U8, align_bytes=64)
+            nc.vector.quantize_mx(
+                out=g_codes[:].bitcast(E5M2X4),
+                scales=g_scales[:],
+                in_=grouped[:, 0:B].rearrange("p w t -> p (w t)"),
+            )
+            w_codes = mx_pool.tile([P, KRON], U32, align_bytes=64)
+            w_scales = mx_pool.tile([P, KRON], U8, align_bytes=64)
+            nc.vector.quantize_mx(
+                out=w_codes[:].bitcast(E4M3X4),
+                scales=w_scales[:],
+                in_=grouped[:, B : B + KRON].rearrange("p w t -> p (w t)"),
+            )
+            operands = (g_codes, g_scales, w_codes, w_scales)
+        multiply(PASSES - 1, *operands)
 
         zT = const.tile([P, N_TILES, ORD * R], F32)
         nc.scalar.copy(out=zT[:], in_=zT_ps[:, :, 0 : ORD * R])

@@ -27,6 +27,7 @@ N_TILES = B // P
 G_PE = 112
 W_PE = 80
 G_SBUF = B - G_PE
+Z_PASS = PASSES // 2
 RUN = 4
 
 FLOPS = 2 * Q * KRON * B
@@ -70,8 +71,6 @@ def tile_fast_tucker_taylor_pa_k_kernel(tc, z, G2, grad_out, out):
         nc.vector.memset(z_rows[:], 0.0)
         nc.scalar.dma_start(out=z_rows[0 : ORD * R, :], in_=z.rearrange("o r n -> (o r) n"))
         zT_ps = psum.tile([P, N_TILES, P], BF16)
-        for j in range(N_TILES):
-            nc.tensor.transpose(zT_ps[:, j, :], z_rows[:, j * P : (j + 1) * P], ident_bf[:])
 
         res = tail.tile([P, P], F32)
         nc.vector.memset(res[:], 0.0)
@@ -105,6 +104,9 @@ def tile_fast_tucker_taylor_pa_k_kernel(tc, z, G2, grad_out, out):
             regroup_on_tensor(nc, ident_bf[:], w_raw[:, :, 0:W_PE], moved[:, G_PE : G_PE + W_PE])
             if c > 0:
                 multiply(c - 1, *operands)
+            if c == Z_PASS:
+                for j in range(N_TILES):
+                    nc.tensor.transpose(zT_ps[:, j, :], z_rows[:, j * P : (j + 1) * P], ident_bf[:])
 
             regroup(nc.scalar.copy, g_raw[:, :, 0:G_SBUF], grouped[:, 0:G_SBUF])
             nc.scalar.copy(out=grouped[:, G_SBUF : B + W_PE], in_=moved[:])

@@ -28,6 +28,7 @@ G_PE = 112
 W_PE = 80
 G_SBUF = B - G_PE
 Z_PASS = PASSES // 2
+LEAD = 2
 RUN = 4
 
 FLOPS = 2 * Q * KRON * B
@@ -61,7 +62,7 @@ def tile_fast_tucker_taylor_pa_k_kernel(tc, z, G2, grad_out, out):
         mx_pool = ctx.enter_context(tc.tile_pool(name="mx", bufs=5))
         tail = ctx.enter_context(tc.tile_pool(name="tail", bufs=1))
         psum = ctx.enter_context(tc.psum_pool(name="psum", bufs=1))
-        move_psum = ctx.enter_context(tc.psum_pool(name="move_psum", bufs=2))
+        move_psum = ctx.enter_context(tc.psum_pool(name="move_psum", bufs=3))
 
         ident_bf = const.tile([P, P], BF16)
         make_identity(nc, ident_bf[:])
@@ -90,7 +91,7 @@ def tile_fast_tucker_taylor_pa_k_kernel(tc, z, G2, grad_out, out):
                     stop=(c == PASSES - 1),
                 )
 
-        operands = None
+        operands = {}
         for c in range(PASSES):
             rows = slice(c * K_PASS, (c + 1) * K_PASS)
             g_raw = raw_pool.tile([P, PACK, B], BF16)
@@ -102,8 +103,8 @@ def tile_fast_tucker_taylor_pa_k_kernel(tc, z, G2, grad_out, out):
             moved = move_psum.tile([P, G_PE + W_PE, PACK], BF16)
             regroup_on_tensor(nc, ident_bf[:], g_raw[:, :, G_SBUF:B], moved[:, 0:G_PE])
             regroup_on_tensor(nc, ident_bf[:], w_raw[:, :, 0:W_PE], moved[:, G_PE : G_PE + W_PE])
-            if c > 0:
-                multiply(c - 1, *operands)
+            if c >= LEAD:
+                multiply(c - LEAD, *operands.pop(c - LEAD))
             if c == Z_PASS:
                 for j in range(N_TILES):
                     nc.tensor.transpose(zT_ps[:, j, :], z_rows[:, j * P : (j + 1) * P], ident_bf[:])
@@ -126,8 +127,9 @@ def tile_fast_tucker_taylor_pa_k_kernel(tc, z, G2, grad_out, out):
                 scales=w_scales[:],
                 in_=grouped[:, B : B + KRON].rearrange("p w t -> p (w t)"),
             )
-            operands = (g_codes, g_scales, w_codes, w_scales)
-        multiply(PASSES - 1, *operands)
+            operands[c] = (g_codes, g_scales, w_codes, w_scales)
+        for c in range(PASSES - LEAD, PASSES):
+            multiply(c, *operands.pop(c))
 
         zT = const.tile([P, N_TILES, ORD * R], F32)
         nc.scalar.copy(out=zT[:], in_=zT_ps[:, :, 0 : ORD * R])
@@ -198,7 +200,7 @@ def tile_fast_tucker_taylor_pa_k_kernel(tc, z, G2, grad_out, out):
             op=ADD,
         )
 
-        resT_ps = psum.tile([P, P], F32)
+        resT_ps = move_psum.tile([P, P], F32, name="moved")
         nc.tensor.transpose(resT_ps[:], res[:], ident_f32[:])
         resT = tail.tile([P, P], F32)
         nc.vector.tensor_copy(out=resT[:], in_=resT_ps[:])

@@ -42,14 +42,13 @@ def regroup(copy, raw, grouped):
 
 
 def regroup_on_tensor(nc, ident, raw, grouped):
-    for t in range(0, PACK, 2):
-        nc.tensor.matmul(
-            out=grouped[:, :, t : t + 2],
-            lhsT=ident,
-            rhs=raw[:, t : t + 2, :].rearrange("p t w -> p w t"),
-            start=True,
-            stop=True,
-        )
+    nc.tensor.matmul(
+        out=grouped.rearrange("p w t -> p t w"),
+        lhsT=ident,
+        rhs=raw,
+        start=True,
+        stop=True,
+    )
 
 
 def tile_fast_tucker_taylor_pa_k_kernel(tc, z, G2, grad_out, out):
@@ -139,15 +138,16 @@ def tile_fast_tucker_taylor_pa_k_kernel(tc, z, G2, grad_out, out):
 
         prod_a = tail.tile([P, N_TILES, R * R, R], F32)
         scaled = tail.tile([P, N_TILES, R, R * R], F32)
-        for i in range(N_TILES):
-            j = (i + 1) % N_TILES
+
+        def multiply_by_z0(j):
             nc.vector.tensor_tensor(
                 out=prod_a[:, j],
                 in0=acc[j][:].rearrange("p (f a) -> p f a", a=R),
                 in1=z0[:, j].unsqueeze(1).to_broadcast([P, R * R, R]),
                 op=MULT,
             )
-            j = i
+
+        def scale_by_z2(j):
             for c in range(R):
                 nc.scalar.activation(
                     out=scaled[:, j, c],
@@ -155,50 +155,64 @@ def tile_fast_tucker_taylor_pa_k_kernel(tc, z, G2, grad_out, out):
                     func=COPY,
                     scale=z2[:, j, c : c + 1],
                 )
+
+        multiply_by_z0(0)
+        scale_by_z2(1)
+        multiply_by_z0(2)
+        scale_by_z2(0)
+        multiply_by_z0(3)
+        scale_by_z2(2)
+        multiply_by_z0(1)
+        scale_by_z2(3)
+
         u = tail.tile([P, N_TILES, R, R], F32)
-        nc.vector.tensor_reduce(
-            out=u[:].rearrange("p j c b -> p (j c b)"),
-            in_=prod_a[:].rearrange("p j f a -> p (j f) a"),
-            axis=X,
-            op=ADD,
-        )
-        pieces = R
-        while pieces > 1:
-            pieces = pieces // 2
+        t = scaled[:, :, 0].rearrange("p j (b a) -> p j b a", a=R)
+        pairs = tail.tile([P, ORD, R, N_TILES, R], F32)
+
+        def sum_over_a(first, end):
+            nc.vector.tensor_reduce(
+                out=u[:, first:end].rearrange("p j c b -> p (j c b)"),
+                in_=prod_a[:, first:end].rearrange("p j f a -> p (j f) a"),
+                axis=X,
+                op=ADD,
+            )
+
+        def add_pieces(pieces):
             nc.vector.tensor_tensor(
                 out=scaled[:, :, 0:pieces],
                 in0=scaled[:, :, 0:pieces],
                 in1=scaled[:, :, pieces : 2 * pieces],
                 op=ADD,
             )
-        t = scaled[:, :, 0].rearrange("p j (b a) -> p j b a", a=R)
 
-        pairs = tail.tile([P, ORD, R, N_TILES, R], F32)
-        shape = [P, N_TILES, R, R]
-        nc.vector.tensor_tensor(
-            out=pairs[:, 2].rearrange("p c j b -> p j c b"),
-            in0=u[:],
-            in1=z1.unsqueeze(2).to_broadcast(shape),
-            op=MULT,
-        )
-        nc.vector.tensor_tensor(
-            out=pairs[:, 1].rearrange("p b j c -> p j b c"),
-            in0=u[:].rearrange("p j c b -> p j b c"),
-            in1=z2.unsqueeze(2).to_broadcast(shape),
-            op=MULT,
-        )
-        nc.vector.tensor_tensor(
-            out=pairs[:, 0].rearrange("p a j b -> p j a b"),
-            in0=t.rearrange("p j b a -> p j a b"),
-            in1=z1.unsqueeze(2).to_broadcast(shape),
-            op=MULT,
-        )
-        nc.vector.tensor_reduce(
-            out=res[:, 0 : ORD * R * N_TILES],
-            in_=pairs[:].rearrange("p o r j y -> p (o r j) y"),
-            axis=X,
-            op=ADD,
-        )
+        def multiply_pairs(o, view, first, factors):
+            nc.vector.tensor_tensor(
+                out=pairs[:, o].rearrange(view),
+                in0=first,
+                in1=factors.unsqueeze(2).to_broadcast([P, N_TILES, R, R]),
+                op=MULT,
+            )
+
+        def sum_pairs(first, end):
+            width = R * N_TILES
+            nc.vector.tensor_reduce(
+                out=res[:, first * width : end * width],
+                in_=pairs[:, first:end].rearrange("p o r j y -> p (o r j) y"),
+                axis=X,
+                op=ADD,
+            )
+
+        half = N_TILES // 2
+        sum_over_a(0, half)
+        sum_over_a(half, N_TILES)
+        add_pieces(4)
+        multiply_pairs(2, "p c j b -> p j c b", u[:], z1)
+        add_pieces(2)
+        multiply_pairs(1, "p b j c -> p j b c", u[:].rearrange("p j c b -> p j b c"), z2)
+        add_pieces(1)
+        sum_pairs(1, ORD)
+        multiply_pairs(0, "p a j b -> p j a b", t.rearrange("p j b a -> p j a b"), z1)
+        sum_pairs(0, 1)
 
         resT_ps = move_psum.tile([P, P], F32, name="moved")
         nc.tensor.transpose(resT_ps[:], res[:], ident_f32[:])

@@ -24,8 +24,8 @@ ORD = 3
 KRON = R**ORD
 B = 512
 N_TILES = B // P
-G_PE = 112
-W_PE = 80
+G_PE = 128
+W_PE = 72
 G_SBUF = B - G_PE
 Z_PASS = PASSES // 2
 LEAD = 2
@@ -69,7 +69,6 @@ def tile_fast_tucker_taylor_pa_k_kernel(tc, z, G2, grad_out, out):
         make_identity(nc, ident_f32[:])
         z_rows = const.tile([P, B], BF16)
         nc.vector.memset(z_rows[:], 0.0)
-        nc.scalar.dma_start(out=z_rows[0 : ORD * R, :], in_=z.rearrange("o r n -> (o r) n"))
         zT_ps = psum.tile([P, N_TILES, P], BF16)
 
         res = tail.tile([P, P], F32)
@@ -97,6 +96,9 @@ def tile_fast_tucker_taylor_pa_k_kernel(tc, z, G2, grad_out, out):
             nc.sync.dma_start(out=g_raw[:], in_=grad_out[rows, :].rearrange("(p t) w -> p t w", t=PACK))
             w_raw = raw_pool.tile([P, PACK, KRON], BF16)
             nc.sync.dma_start(out=w_raw[:], in_=G2[rows, :].rearrange("(p t) w -> p t w", t=PACK))
+
+            if c == Z_PASS // 2:
+                nc.sync.dma_start(out=z_rows[0 : ORD * R, :], in_=z.rearrange("o r n -> (o r) n"))
 
             grouped = grouped_pool.tile([P, B + KRON, PACK], BF16, align_bytes=64)
             moved = move_psum.tile([P, G_PE + W_PE, PACK], BF16)
@@ -177,11 +179,11 @@ def tile_fast_tucker_taylor_pa_k_kernel(tc, z, G2, grad_out, out):
                 op=ADD,
             )
 
-        def add_pieces(pieces):
-            nc.vector.tensor_tensor(
-                out=scaled[:, :, 0:pieces],
-                in0=scaled[:, :, 0:pieces],
-                in1=scaled[:, :, pieces : 2 * pieces],
+        def add_pieces(engine, first, end, pieces):
+            engine.tensor_tensor(
+                out=scaled[:, first:end, 0:pieces],
+                in0=scaled[:, first:end, 0:pieces],
+                in1=scaled[:, first:end, pieces : 2 * pieces],
                 op=ADD,
             )
 
@@ -203,13 +205,15 @@ def tile_fast_tucker_taylor_pa_k_kernel(tc, z, G2, grad_out, out):
             )
 
         half = N_TILES // 2
+        for pieces in (4, 2, 1):
+            add_pieces(nc.gpsimd, 0, half, pieces)
         sum_over_a(0, half)
         sum_over_a(half, N_TILES)
-        add_pieces(4)
+        add_pieces(nc.vector, half, N_TILES, 4)
         multiply_pairs(2, "p c j b -> p j c b", u[:], z1)
-        add_pieces(2)
+        add_pieces(nc.vector, half, N_TILES, 2)
         multiply_pairs(1, "p b j c -> p j b c", u[:].rearrange("p j c b -> p j b c"), z2)
-        add_pieces(1)
+        add_pieces(nc.vector, half, N_TILES, 1)
         sum_pairs(1, ORD)
         multiply_pairs(0, "p a j b -> p j a b", t.rearrange("p j b a -> p j a b"), z1)
         sum_pairs(0, 1)

@@ -24,8 +24,8 @@ ORD = 3
 KRON = R**ORD
 B = 512
 N_TILES = B // P
-G_PE = 128
-W_PE = 72
+G_PE = 120
+W_PE = 80
 G_SBUF = B - G_PE
 Z_PASS = PASSES // 2
 LEAD = 2
@@ -116,18 +116,30 @@ def tile_fast_tucker_taylor_pa_k_kernel(tc, z, G2, grad_out, out):
 
             g_codes = mx_pool.tile([P, B], U32, align_bytes=64)
             g_scales = mx_pool.tile([P, B], U8, align_bytes=64)
-            nc.vector.quantize_mx(
-                out=g_codes[:].bitcast(E5M2X4),
-                scales=g_scales[:],
-                in_=grouped[:, 0:B].rearrange("p w t -> p (w t)"),
-            )
             w_codes = mx_pool.tile([P, KRON], U32, align_bytes=64)
             w_scales = mx_pool.tile([P, KRON], U8, align_bytes=64)
-            nc.vector.quantize_mx(
-                out=w_codes[:].bitcast(E4M3X4),
-                scales=w_scales[:],
-                in_=grouped[:, B : B + KRON].rearrange("p w t -> p (w t)"),
-            )
+
+            def quantize_g(cols):
+                nc.vector.quantize_mx(
+                    out=g_codes[:, cols].bitcast(E5M2X4),
+                    scales=g_scales[:, cols],
+                    in_=grouped[:, cols].rearrange("p w t -> p (w t)"),
+                )
+
+            def quantize_w():
+                nc.vector.quantize_mx(
+                    out=w_codes[:].bitcast(E4M3X4),
+                    scales=w_scales[:],
+                    in_=grouped[:, B : B + KRON].rearrange("p w t -> p (w t)"),
+                )
+
+            if c < PASSES - 1:
+                quantize_g(slice(0, B))
+                quantize_w()
+            else:
+                quantize_w()
+                quantize_g(slice(0, B // 2))
+                quantize_g(slice(B // 2, B))
             operands[c] = (g_codes, g_scales, w_codes, w_scales)
         for c in range(PASSES - LEAD, PASSES):
             multiply(c, *operands.pop(c))
@@ -179,11 +191,11 @@ def tile_fast_tucker_taylor_pa_k_kernel(tc, z, G2, grad_out, out):
                 op=ADD,
             )
 
-        def add_pieces(engine, first, end, pieces):
-            engine.tensor_tensor(
-                out=scaled[:, first:end, 0:pieces],
-                in0=scaled[:, first:end, 0:pieces],
-                in1=scaled[:, first:end, pieces : 2 * pieces],
+        def add_pieces(pieces):
+            nc.vector.tensor_tensor(
+                out=scaled[:, :, 0:pieces],
+                in0=scaled[:, :, 0:pieces],
+                in1=scaled[:, :, pieces : 2 * pieces],
                 op=ADD,
             )
 
@@ -205,15 +217,13 @@ def tile_fast_tucker_taylor_pa_k_kernel(tc, z, G2, grad_out, out):
             )
 
         half = N_TILES // 2
-        for pieces in (4, 2, 1):
-            add_pieces(nc.gpsimd, 0, half, pieces)
         sum_over_a(0, half)
         sum_over_a(half, N_TILES)
-        add_pieces(nc.vector, half, N_TILES, 4)
+        add_pieces(4)
         multiply_pairs(2, "p c j b -> p j c b", u[:], z1)
-        add_pieces(nc.vector, half, N_TILES, 2)
+        add_pieces(2)
         multiply_pairs(1, "p b j c -> p j b c", u[:].rearrange("p j c b -> p j b c"), z2)
-        add_pieces(nc.vector, half, N_TILES, 1)
+        add_pieces(1)
         sum_pairs(1, ORD)
         multiply_pairs(0, "p a j b -> p j a b", t.rearrange("p j b a -> p j a b"), z1)
         sum_pairs(0, 1)

@@ -24,7 +24,7 @@ ORD = 3
 KRON = R**ORD
 B = 512
 N_TILES = B // P
-G_PE = 120
+G_PE = 116
 W_PE = 80
 G_SBUF = B - G_PE
 Z_PASS = PASSES // 2
@@ -180,7 +180,12 @@ def tile_fast_tucker_taylor_pa_k_kernel(tc, z, G2, grad_out, out):
         scale_by_z2(3)
 
         u = tail.tile([P, N_TILES, R, R], F32)
-        t = scaled[:, :, 0].rearrange("p j (b a) -> p j b a", a=R)
+        half = N_TILES // 2
+        t_ps = move_psum.tile([P, half, R * R], F32, name="moved")
+        for c in range(R):
+            nc.tensor.matmul(out=t_ps[:], lhsT=ident_f32[:], rhs=scaled[:, 0:half, c], start=(c == 0), stop=(c == R - 1))
+        t_first = t_ps[:].rearrange("p j (b a) -> p j a b", a=R)
+        t_second = scaled[:, half:, 0].rearrange("p j (b a) -> p j a b", a=R)
         pairs = tail.tile([P, ORD, R, N_TILES, R], F32)
 
         def sum_over_a(first, end):
@@ -193,17 +198,17 @@ def tile_fast_tucker_taylor_pa_k_kernel(tc, z, G2, grad_out, out):
 
         def add_pieces(pieces):
             nc.vector.tensor_tensor(
-                out=scaled[:, :, 0:pieces],
-                in0=scaled[:, :, 0:pieces],
-                in1=scaled[:, :, pieces : 2 * pieces],
+                out=scaled[:, half:, 0:pieces],
+                in0=scaled[:, half:, 0:pieces],
+                in1=scaled[:, half:, pieces : 2 * pieces],
                 op=ADD,
             )
 
-        def multiply_pairs(o, view, first, factors):
+        def multiply_pairs(products, view, first, factors):
             nc.vector.tensor_tensor(
-                out=pairs[:, o].rearrange(view),
+                out=products.rearrange(view),
                 in0=first,
-                in1=factors.unsqueeze(2).to_broadcast([P, N_TILES, R, R]),
+                in1=factors.unsqueeze(2).to_broadcast([P, first.shape[1], R, R]),
                 op=MULT,
             )
 
@@ -216,23 +221,22 @@ def tile_fast_tucker_taylor_pa_k_kernel(tc, z, G2, grad_out, out):
                 op=ADD,
             )
 
-        half = N_TILES // 2
         sum_over_a(0, half)
         sum_over_a(half, N_TILES)
         add_pieces(4)
-        multiply_pairs(2, "p c j b -> p j c b", u[:], z1)
+        multiply_pairs(pairs[:, 2], "p c j b -> p j c b", u[:], z1)
         add_pieces(2)
-        multiply_pairs(1, "p b j c -> p j b c", u[:].rearrange("p j c b -> p j b c"), z2)
+        multiply_pairs(pairs[:, 1], "p b j c -> p j b c", u[:].rearrange("p j c b -> p j b c"), z2)
         add_pieces(1)
+        multiply_pairs(pairs[:, 0, :, 0:half], "p a j b -> p j a b", t_first, z1[:, 0:half])
+        multiply_pairs(pairs[:, 0, :, half:], "p a j b -> p j a b", t_second, z1[:, half:])
         sum_pairs(1, ORD)
-        multiply_pairs(0, "p a j b -> p j a b", t.rearrange("p j b a -> p j a b"), z1)
         sum_pairs(0, 1)
 
         resT_ps = move_psum.tile([P, P], F32, name="moved")
         nc.tensor.transpose(resT_ps[:], res[:], ident_f32[:])
         resT = tail.tile([P, P], F32)
         nc.vector.tensor_copy(out=resT[:], in_=resT_ps[:])
-        nc.sync.dma_start(
-            out=out.rearrange("o r (j n) -> (o r j) n", j=N_TILES),
-            in_=resT[0 : ORD * R * N_TILES, :],
-        )
+        out_rows = out.rearrange("o r (j n) -> (o r j) n", j=N_TILES)
+        nc.sync.dma_start(out=out_rows[0 : P // 2], in_=resT[0 : P // 2, :])
+        nc.scalar.dma_start(out=out_rows[P // 2 :], in_=resT[P // 2 : ORD * R * N_TILES, :])

from contextlib import ExitStack

import concourse.mybir as mybir
from concourse.masks import make_identity

BF16 = mybir.dt.bfloat16
F32 = mybir.dt.float32
U32 = mybir.dt.uint32
U8 = mybir.dt.uint8
E4M3X4 = mybir.dt.float8_e4m3fn_x4
E5M2X4 = mybir.dt.float8_e5m2_x4
MULT = mybir.AluOpType.mult
ADD = mybir.AluOpType.add
X = mybir.AxisListType.X
COPY = mybir.ActivationFunctionType.Copy

P = 128
PACK = 4
K_PASS = P * PACK
Q = 16384
PASSES = Q // K_PASS
R = 8
ORD = 3
KRON = R**ORD
B = 512
N_TILES = B // P
G_PE = 116
W_PE = 80
G_SBUF = B - G_PE
Z_PASS = PASSES // 2
LEAD = 2
RUN = 4

FLOPS = 2 * Q * KRON * B


def regroup(copy, raw, grouped):
    copy(
        out=grouped.rearrange("p (g i) t -> p g t i", i=RUN),
        in_=raw.rearrange("p t (g i) -> p g t i", i=RUN),
    )


def regroup_on_tensor(nc, ident, raw, grouped):
    nc.tensor.matmul(
        out=grouped.rearrange("p w t -> p t w"),
        lhsT=ident,
        rhs=raw,
        start=True,
        stop=True,
    )


def tile_fast_tucker_taylor_pa_k_kernel(tc, z, G2, grad_out, out):
    nc = tc.nc
    with ExitStack() as ctx:
        ctx.enter_context(tc.manual_schedule())
        const = ctx.enter_context(tc.tile_pool(name="const", bufs=1))
        raw_pool = ctx.enter_context(tc.tile_pool(name="raw", bufs=8))
        grouped_pool = ctx.enter_context(tc.tile_pool(name="grouped", bufs=5))
        mx_pool = ctx.enter_context(tc.tile_pool(name="mx", bufs=5))
        tail = ctx.enter_context(tc.tile_pool(name="tail", bufs=1))
        psum = ctx.enter_context(tc.psum_pool(name="psum", bufs=1))
        move_psum = ctx.enter_context(tc.psum_pool(name="move_psum", bufs=3))

        ident_bf = const.tile([P, P], BF16)
        make_identity(nc, ident_bf[:])
        ident_f32 = const.tile([P, P], F32)
        make_identity(nc, ident_f32[:])
        z_rows = const.tile([P, B], BF16)
        nc.vector.memset(z_rows[:], 0.0)
        zT_ps = psum.tile([P, N_TILES, P], BF16)

        res = tail.tile([P, P], F32)
        nc.vector.memset(res[:], 0.0)

        acc = [psum.tile([P, KRON], F32, name="acc%d" % j) for j in range(N_TILES)]

        def multiply(c, g_codes, g_scales, w_codes, w_scales):
            for j in range(N_TILES):
                n_cols = slice(j * P, (j + 1) * P)
                nc.tensor.matmul_mx(
                    out=acc[j][:],
                    lhsT=g_codes[:, n_cols].bitcast(E5M2X4),
                    lhsT_scale=g_scales[:, n_cols],
                    rhs=w_codes[:].bitcast(E4M3X4),
                    rhs_scale=w_scales[:],
                    start=(c == 0),
                    stop=(c == PASSES - 1),
                )

        operands = {}
        for c in range(PASSES):
            rows = slice(c * K_PASS, (c + 1) * K_PASS)
            g_raw = raw_pool.tile([P, PACK, B], BF16)
            nc.sync.dma_start(out=g_raw[:], in_=grad_out[rows, :].rearrange("(p t) w -> p t w", t=PACK))
            w_raw = raw_pool.tile([P, PACK, KRON], BF16)
            nc.sync.dma_start(out=w_raw[:], in_=G2[rows, :].rearrange("(p t) w -> p t w", t=PACK))

            if c == Z_PASS // 2:
                nc.sync.dma_start(out=z_rows[0 : ORD * R, :], in_=z.rearrange("o r n -> (o r) n"))

            grouped = grouped_pool.tile([P, B + KRON, PACK], BF16, align_bytes=64)
            moved = move_psum.tile([P, G_PE + W_PE, PACK], BF16)
            regroup_on_tensor(nc, ident_bf[:], g_raw[:, :, G_SBUF:B], moved[:, 0:G_PE])
            regroup_on_tensor(nc, ident_bf[:], w_raw[:, :, 0:W_PE], moved[:, G_PE : G_PE + W_PE])
            if c >= LEAD:
                multiply(c - LEAD, *operands.pop(c - LEAD))
            if c == Z_PASS:
                for j in range(N_TILES):
                    nc.tensor.transpose(zT_ps[:, j, :], z_rows[:, j * P : (j + 1) * P], ident_bf[:])

            regroup(nc.scalar.copy, g_raw[:, :, 0:G_SBUF], grouped[:, 0:G_SBUF])
            nc.scalar.copy(out=grouped[:, G_SBUF : B + W_PE], in_=moved[:])
            regroup(nc.vector.tensor_copy, w_raw[:, :, W_PE:KRON], grouped[:, B + W_PE : B + KRON])

            g_codes = mx_pool.tile([P, B], U32, align_bytes=64)
            g_scales = mx_pool.tile([P, B], U8, align_bytes=64)
            w_codes = mx_pool.tile([P, KRON], U32, align_bytes=64)
            w_scales = mx_pool.tile([P, KRON], U8, align_bytes=64)

            def quantize_g(cols):
                nc.vector.quantize_mx(
                    out=g_codes[:, cols].bitcast(E5M2X4),
                    scales=g_scales[:, cols],
                    in_=grouped[:, cols].rearrange("p w t -> p (w t)"),
                )

            def quantize_w():
                nc.vector.quantize_mx(
                    out=w_codes[:].bitcast(E4M3X4),
                    scales=w_scales[:],
                    in_=grouped[:, B : B + KRON].rearrange("p w t -> p (w t)"),
                )

            if c < PASSES - 1:
                quantize_g(slice(0, B))
                quantize_w()
            else:
                quantize_w()
                quantize_g(slice(0, B // 2))
                quantize_g(slice(B // 2, B))
            operands[c] = (g_codes, g_scales, w_codes, w_scales)
        for c in range(PASSES - LEAD, PASSES):
            multiply(c, *operands.pop(c))

        zT = const.tile([P, N_TILES, ORD * R], F32)
        nc.scalar.copy(out=zT[:], in_=zT_ps[:, :, 0 : ORD * R])
        z0 = zT[:, :, 0:R]
        z1 = zT[:, :, R : 2 * R]
        z2 = zT[:, :, 2 * R : 3 * R]

        prod_a = tail.tile([P, N_TILES, R * R, R], F32)
        scaled = tail.tile([P, N_TILES, R, R * R], F32)

        def multiply_by_z0(j):
            nc.vector.tensor_tensor(
                out=prod_a[:, j],
                in0=acc[j][:].rearrange("p (f a) -> p f a", a=R),
                in1=z0[:, j].unsqueeze(1).to_broadcast([P, R * R, R]),
                op=MULT,
            )

        def scale_by_z2(j):
            for c in range(R):
                nc.scalar.activation(
                    out=scaled[:, j, c],
                    in_=acc[j][:, c * R * R : (c + 1) * R * R],
                    func=COPY,
                    scale=z2[:, j, c : c + 1],
                )

        multiply_by_z0(0)
        scale_by_z2(1)
        multiply_by_z0(2)
        scale_by_z2(0)
        multiply_by_z0(3)
        scale_by_z2(2)
        multiply_by_z0(1)
        scale_by_z2(3)

        u = tail.tile([P, N_TILES, R, R], F32)
        half = N_TILES // 2
        t_ps = move_psum.tile([P, half, R * R], F32, name="moved")
        for c in range(R):
            nc.tensor.matmul(out=t_ps[:], lhsT=ident_f32[:], rhs=scaled[:, 0:half, c], start=(c == 0), stop=(c == R - 1))
        t_first = t_ps[:].rearrange("p j (b a) -> p j a b", a=R)
        t_second = scaled[:, half:, 0].rearrange("p j (b a) -> p j a b", a=R)
        pairs = tail.tile([P, ORD, R, N_TILES, R], F32)

        def sum_over_a(first, end):
            nc.vector.tensor_reduce(
                out=u[:, first:end].rearrange("p j c b -> p (j c b)"),
                in_=prod_a[:, first:end].rearrange("p j f a -> p (j f) a"),
                axis=X,
                op=ADD,
            )

        def add_pieces(pieces):
            nc.vector.tensor_tensor(
                out=scaled[:, half:, 0:pieces],
                in0=scaled[:, half:, 0:pieces],
                in1=scaled[:, half:, pieces : 2 * pieces],
                op=ADD,
            )

        def multiply_pairs(products, view, first, factors):
            nc.vector.tensor_tensor(
                out=products.rearrange(view),
                in0=first,
                in1=factors.unsqueeze(2).to_broadcast([P, first.shape[1], R, R]),
                op=MULT,
            )

        def sum_pairs(first, end):
            width = R * N_TILES
            nc.vector.tensor_reduce(
                out=res[:, first * width : end * width],
                in_=pairs[:, first:end].rearrange("p o r j y -> p (o r j) y"),
                axis=X,
                op=ADD,
            )

        sum_over_a(0, half)
        sum_over_a(half, N_TILES)
        add_pieces(4)
        multiply_pairs(pairs[:, 2], "p c j b -> p j c b", u[:], z1)
        add_pieces(2)
        multiply_pairs(pairs[:, 1], "p b j c -> p j b c", u[:].rearrange("p j c b -> p j b c"), z2)
        add_pieces(1)
        multiply_pairs(pairs[:, 0, :, 0:half], "p a j b -> p j a b", t_first, z1[:, 0:half])
        multiply_pairs(pairs[:, 0, :, half:], "p a j b -> p j a b", t_second, z1[:, half:])
        sum_pairs(1, ORD)
        sum_pairs(0, 1)

        resT_ps = move_psum.tile([P, P], F32, name="moved")
        nc.tensor.transpose(resT_ps[:], res[:], ident_f32[:])
        resT = tail.tile([P, P], F32)
        nc.vector.tensor_copy(out=resT[:], in_=resT_ps[:])
        out_rows = out.rearrange("o r (j n) -> (o r j) n", j=N_TILES)
        nc.sync.dma_start(out=out_rows[0 : P // 2], in_=resT[0 : P // 2, :])
        nc.scalar.dma_start(out=out_rows[P // 2 :], in_=resT[P // 2 : ORD * R * N_TILES, :])
